import numpy as np
import ml_dtypes


def mxq(x, axis, fmt="e4m3"):
    dtype, down = {"e4m3": (ml_dtypes.float8_e4m3fn, 7), "e5m2": (ml_dtypes.float8_e5m2, 14)}[fmt]
    v = np.moveaxis(np.asarray(x, np.float32).astype(ml_dtypes.bfloat16).astype(np.float64), axis, -1)
    blocks = v.reshape(v.shape[:-1] + (-1, 32))
    amax = np.abs(blocks).max(-1, keepdims=True)
    byte = np.maximum(np.where(amax > 0, np.frexp(amax)[1] - 1 + 127, 0) - down, 1)
    scale = np.exp2(byte - 127.0)
    codes = (blocks / scale).astype(np.float32).astype(dtype).astype(np.float64)
    return np.moveaxis((codes * scale).reshape(v.shape), -1, axis)


WIDE = False


def mx_kscale(k):
    if not WIDE:
        return np.ones(k)
    levels = np.array([10, -10, 5, -5, 0])
    a = np.random.permutation(np.resize(levels, k // 512 * 4)).reshape(k // 512, 4)
    idx = np.arange(k)
    return np.exp2(a[idx // 512, idx % 128 // 32])


BF16 = ml_dtypes.bfloat16


def bf(x):
    return np.asarray(x, np.float32).astype(BF16)


def f64(x):
    return np.asarray(x).astype(np.float64)


B, NB, NL, NG, NK = 128, 512, 1536, 500, 3
N2 = 2 * NB


def setup_inputs():
    s = mx_kscale(N2)
    r = s[:NB]
    return {'Volt': bf(np.random.standard_normal((B, N2)) * s),
            'Y_top': bf(np.random.standard_normal((NB, N2)) * 4.0 / np.sqrt(N2) / s[None, :] / r[:, None]),
            'Yconj_top': bf(np.random.standard_normal((NB, N2)) * 4.0 / np.sqrt(N2) / s[None, :] / r[:, None]),
            'PQ_Loads': bf(np.random.standard_normal((B, N2))),
            'PQ_Gens': bf(np.random.standard_normal((B, N2)))}


def reference(Volt, Y_top, Yconj_top, PQ_Loads, PQ_Gens):
    V = f64(Volt)
    Vq = mxq(V, 1, 'e4m3')
    YV = Vq @ mxq(f64(Y_top), 1, 'e4m3').T
    YcV = Vq @ mxq(f64(Yconj_top), 1, 'e4m3').T
    out = np.sum(V[:, :NB] * YV, axis=1) + np.sum(V[:, :NB] * YcV, axis=1)
    pq = f64(PQ_Loads) - f64(PQ_Gens)
    return out + np.sum(pq[:, :NB], axis=1) + np.sum(pq[:, NB:], axis=1)

@@ -1,0 +1,134 @@
+from contextlib import ExitStack
+
+import concourse.mybir as mybir
+from concourse.masks import make_identity
+
+F32 = mybir.dt.float32
+BF16 = mybir.dt.bfloat16
+U32 = mybir.dt.uint32
+U8 = mybir.dt.uint8
+FP8X4 = mybir.dt.float8_e4m3fn_x4
+MULT = mybir.AluOpType.mult
+ADD = mybir.AluOpType.add
+
+P = 128
+K = 1024
+NB = 512
+K_PASS = 512
+PASSES = K // K_PASS
+ROUNDS = NB // P
+BLOCKS = 1 + 2 * ROUNDS
+AHEAD = 2
+
+FLOPS = 2 * 2 * P * NB * K
+
+
+def tile_kktloss_pc_s_kernel(tc, Volt, Y_top, Yconj_top, PQ_Loads, PQ_Gens, out):
+    nc = tc.nc
+    with ExitStack() as ctx:
+        consts = ctx.enter_context(tc.tile_pool(name="consts", bufs=1))
+        loads = ctx.enter_context(tc.tile_pool(name="loads", bufs=1))
+        stage = ctx.enter_context(tc.tile_pool(name="stage", bufs=AHEAD + 2))
+        keep = ctx.enter_context(tc.tile_pool(name="keep", bufs=1))
+        small = ctx.enter_context(tc.tile_pool(name="small", bufs=1))
+        flip_psum = ctx.enter_context(tc.psum_pool(name="flip_psum", bufs=4))
+        acc_psum = ctx.enter_context(tc.psum_pool(name="acc_psum", bufs=2))
+        row_psum = ctx.enter_context(tc.psum_pool(name="row_psum", bufs=1))
+        ctx.enter_context(tc.manual_schedule())
+
+        ident = consts.tile([P, P], F32)
+        make_identity(nc, ident[:])
+
+        sources = [Volt[:, :]]
+        for t in range(ROUNDS):
+            sources.append(Y_top[t * P : (t + 1) * P, :])
+            sources.append(Yconj_top[t * P : (t + 1) * P, :])
+        rows_sb = []
+        for j in range(BLOCKS):
+            block = loads.tile([P, K], BF16, name="rows%d" % j)
+            nc.sync.dma_start(out=block[:], in_=sources[j])
+            rows_sb.append(block)
+        volt_sb = rows_sb[0]
+        loads_sb = loads.tile([P, K], BF16)
+        nc.sync.dma_start(out=loads_sb[:], in_=PQ_Loads[:, :])
+        gens_sb = loads.tile([P, K], BF16)
+        nc.sync.dma_start(out=gens_sb[:], in_=PQ_Gens[:, :])
+
+        codes = keep.tile([P, BLOCKS, PASSES * P], U32, align_bytes=64)
+        scales = keep.tile([P, BLOCKS, PASSES * P], U8, align_bytes=64)
+        parts = small.tile([P, ROUNDS + 1], F32)
+        grouped = {}
+
+        def flip(j):
+            words = rows_sb[j][:].bitcast(F32)
+            flipped = flip_psum.tile([P, 2 * PASSES, P], F32)
+            for s in range(2 * PASSES):
+                nc.tensor.transpose(flipped[:, s, :], words[:, s * P : (s + 1) * P], ident[:])
+            grouped[j] = stage.tile([P, K], BF16, align_bytes=64, name="grouped")
+            nc.scalar.copy(
+                out=grouped[j][:].bitcast(F32).rearrange("p (g r u) -> p g r u", g=PASSES, u=2),
+                in_=flipped[:].rearrange("p (g u) r -> p g r u", u=2),
+            )
+
+        def quantise(j):
+            nc.vector.quantize_mx(
+                out=codes[:, j, :].bitcast(FP8X4), scales=scales[:, j, :], in_=grouped[j][:]
+            )
+
+        def multiply(t):
+            acc = acc_psum.tile([P, P], F32)
+            for which in range(2):
+                j = 1 + 2 * t + which
+                for g in range(PASSES):
+                    cols = slice(g * P, (g + 1) * P)
+                    nc.tensor.matmul_mx(
+                        out=acc[:],
+                        lhsT=codes[:, 0, cols].bitcast(FP8X4),
+                        lhsT_scale=scales[:, 0, cols],
+                        rhs=codes[:, j, cols].bitcast(FP8X4),
+                        rhs_scale=scales[:, j, cols],
+                        start=(which == 0 and g == 0),
+                        stop=(which == 1 and g == PASSES - 1),
+                    )
+            weighted = stage.tile([P, P], F32)
+            nc.vector.scalar_tensor_tensor(
+                out=weighted[:],
+                in0=acc[:],
+                scalar=1.0,
+                in1=volt_sb[:, t * P : (t + 1) * P],
+                op0=MULT,
+                op1=MULT,
+                accum_out=parts[:, t : t + 1],
+            )
+
+        def balance():
+            difference = small.tile([P, K], F32)
+            nc.vector.scalar_tensor_tensor(
+                out=difference[:],
+                in0=gens_sb[:],
+                scalar=-1.0,
+                in1=loads_sb[:],
+                op0=MULT,
+                op1=ADD,
+                accum_out=parts[:, ROUNDS : ROUNDS + 1],
+            )
+
+        for step in range(BLOCKS + AHEAD):
+            if step < BLOCKS:
+                flip(step)
+            j = step - AHEAD
+            if j >= 0:
+                quantise(j)
+            if j == BLOCKS - 1:
+                balance()
+            if j >= 2 and j % 2 == 0:
+                multiply(j // 2 - 1)
+
+        total = small.tile([P, 1], F32)
+        nc.vector.tensor_reduce(out=total[:], in_=parts[:], axis=mybir.AxisListType.X, op=ADD)
+
+        row_ps = row_psum.tile([P, P], F32)
+        nc.tensor.transpose(row_ps[:], total[:, 0:1].to_broadcast([P, P]), ident[:])
+        row_sb = small.tile([P, P], F32)
+        nc.vector.tensor_copy(out=row_sb[:], in_=row_ps[:])
+        nc.sync.dma_start(out=out.rearrange("(o b) -> o b", o=1), in_=row_sb[0:1, :])

@@ -7,6 +7,7 @@ F32 = mybir.dt.float32
 BF16 = mybir.dt.bfloat16
 U32 = mybir.dt.uint32
 U8 = mybir.dt.uint8
+I32 = mybir.dt.int32
 FP8X4 = mybir.dt.float8_e4m3fn_x4
 MULT = mybir.AluOpType.mult
 ADD = mybir.AluOpType.add
@@ -19,6 +20,8 @@ PASSES = K // K_PASS
 ROUNDS = NB // P
 BLOCKS = 1 + 2 * ROUNDS
 AHEAD = 2
+WARM_PASSES = 7
+WARM_COLS = 256
 
 FLOPS = 2 * 2 * P * NB * K
 
@@ -34,7 +37,25 @@ def tile_kktloss_pc_s_kernel(tc, Volt, Y_top, Yconj_top, PQ_Loads, PQ_Gens, out)
         flip_psum = ctx.enter_context(tc.psum_pool(name="flip_psum", bufs=4))
         acc_psum = ctx.enter_context(tc.psum_pool(name="acc_psum", bufs=2))
         row_psum = ctx.enter_context(tc.psum_pool(name="row_psum", bufs=1))
+        warm_psum = ctx.enter_context(tc.psum_pool(name="warm_psum", bufs=1))
         ctx.enter_context(tc.manual_schedule())
+
+        zeros = consts.tile([P, 4 * WARM_COLS], BF16, align_bytes=64)
+        zero_codes = consts.tile([P, WARM_COLS], U32, align_bytes=64)
+        zero_scales = consts.tile([P, WARM_COLS], U8, align_bytes=64)
+        nc.vector.memset(zeros[:].bitcast(I32), 0)
+        nc.vector.quantize_mx(out=zero_codes[:].bitcast(FP8X4), scales=zero_scales[:], in_=zeros[:])
+        warm = warm_psum.tile([P, WARM_COLS], F32)
+        for w in range(WARM_PASSES):
+            nc.tensor.matmul_mx(
+                out=warm[:],
+                lhsT=zero_codes[:, 0:P].bitcast(FP8X4),
+                lhsT_scale=zero_scales[:, 0:P],
+                rhs=zero_codes[:].bitcast(FP8X4),
+                rhs_scale=zero_scales[:],
+                start=True,
+                stop=True,
+            )
 
         ident = consts.tile([P, P], F32)
         make_identity(nc, ident[:])

@@ -7,7 +7,6 @@ F32 = mybir.dt.float32
 BF16 = mybir.dt.bfloat16
 U32 = mybir.dt.uint32
 U8 = mybir.dt.uint8
-I32 = mybir.dt.int32
 FP8X4 = mybir.dt.float8_e4m3fn_x4
 MULT = mybir.AluOpType.mult
 ADD = mybir.AluOpType.add
@@ -19,9 +18,8 @@ K_PASS = 512
 PASSES = K // K_PASS
 ROUNDS = NB // P
 BLOCKS = 1 + 2 * ROUNDS
-AHEAD = 2
-WARM_PASSES = 7
-WARM_COLS = 256
+EARLY = ROUNDS - 1
+HALF = K // 2
 
 FLOPS = 2 * 2 * P * NB * K
 
@@ -31,31 +29,12 @@ def tile_kktloss_pc_s_kernel(tc, Volt, Y_top, Yconj_top, PQ_Loads, PQ_Gens, out)
     with ExitStack() as ctx:
         consts = ctx.enter_context(tc.tile_pool(name="consts", bufs=1))
         loads = ctx.enter_context(tc.tile_pool(name="loads", bufs=1))
-        stage = ctx.enter_context(tc.tile_pool(name="stage", bufs=AHEAD + 2))
+        stage = ctx.enter_context(tc.tile_pool(name="stage", bufs=4))
         keep = ctx.enter_context(tc.tile_pool(name="keep", bufs=1))
         small = ctx.enter_context(tc.tile_pool(name="small", bufs=1))
-        flip_psum = ctx.enter_context(tc.psum_pool(name="flip_psum", bufs=4))
-        acc_psum = ctx.enter_context(tc.psum_pool(name="acc_psum", bufs=2))
-        row_psum = ctx.enter_context(tc.psum_pool(name="row_psum", bufs=1))
-        warm_psum = ctx.enter_context(tc.psum_pool(name="warm_psum", bufs=1))
+        flip_psum = ctx.enter_context(tc.psum_pool(name="flip_psum", bufs=5))
+        acc_psum = ctx.enter_context(tc.psum_pool(name="acc_psum", bufs=1))
         ctx.enter_context(tc.manual_schedule())
-
-        zeros = consts.tile([P, 4 * WARM_COLS], BF16, align_bytes=64)
-        zero_codes = consts.tile([P, WARM_COLS], U32, align_bytes=64)
-        zero_scales = consts.tile([P, WARM_COLS], U8, align_bytes=64)
-        nc.vector.memset(zeros[:].bitcast(I32), 0)
-        nc.vector.quantize_mx(out=zero_codes[:].bitcast(FP8X4), scales=zero_scales[:], in_=zeros[:])
-        warm = warm_psum.tile([P, WARM_COLS], F32)
-        for w in range(WARM_PASSES):
-            nc.tensor.matmul_mx(
-                out=warm[:],
-                lhsT=zero_codes[:, 0:P].bitcast(FP8X4),
-                lhsT_scale=zero_scales[:, 0:P],
-                rhs=zero_codes[:].bitcast(FP8X4),
-                rhs_scale=zero_scales[:],
-                start=True,
-                stop=True,
-            )
 
         ident = consts.tile([P, P], F32)
         make_identity(nc, ident[:])
@@ -71,13 +50,15 @@ def tile_kktloss_pc_s_kernel(tc, Volt, Y_top, Yconj_top, PQ_Loads, PQ_Gens, out)
             rows_sb.append(block)
         volt_sb = rows_sb[0]
         loads_sb = loads.tile([P, K], BF16)
-        nc.sync.dma_start(out=loads_sb[:], in_=PQ_Loads[:, :])
         gens_sb = loads.tile([P, K], BF16)
-        nc.sync.dma_start(out=gens_sb[:], in_=PQ_Gens[:, :])
+        for h in range(2):
+            half = slice(h * HALF, (h + 1) * HALF)
+            nc.sync.dma_start(out=loads_sb[:, half], in_=PQ_Loads[:, half])
+            nc.sync.dma_start(out=gens_sb[:, half], in_=PQ_Gens[:, half])
 
         codes = keep.tile([P, BLOCKS, PASSES * P], U32, align_bytes=64)
         scales = keep.tile([P, BLOCKS, PASSES * P], U8, align_bytes=64)
-        parts = small.tile([P, ROUNDS + 1], F32)
+        parts = small.tile([P, 4], F32)
         grouped = {}
 
         def flip(j):
@@ -96,14 +77,13 @@ def tile_kktloss_pc_s_kernel(tc, Volt, Y_top, Yconj_top, PQ_Loads, PQ_Gens, out)
                 out=codes[:, j, :].bitcast(FP8X4), scales=scales[:, j, :], in_=grouped[j][:]
             )
 
-        def multiply(t):
-            acc = acc_psum.tile([P, P], F32)
+        def multiply(t, acc):
             for which in range(2):
                 j = 1 + 2 * t + which
                 for g in range(PASSES):
                     cols = slice(g * P, (g + 1) * P)
                     nc.tensor.matmul_mx(
-                        out=acc[:],
+                        out=acc,
                         lhsT=codes[:, 0, cols].bitcast(FP8X4),
                         lhsT_scale=scales[:, 0, cols],
                         rhs=codes[:, j, cols].bitcast(FP8X4),
@@ -111,44 +91,52 @@ def tile_kktloss_pc_s_kernel(tc, Volt, Y_top, Yconj_top, PQ_Loads, PQ_Gens, out)
                         start=(which == 0 and g == 0),
                         stop=(which == 1 and g == PASSES - 1),
                     )
-            weighted = stage.tile([P, P], F32)
+
+        def weigh(acc, first, width, part):
+            weighted = small.tile([P, width], F32, name="weighted%d" % part)
             nc.vector.scalar_tensor_tensor(
                 out=weighted[:],
-                in0=acc[:],
+                in0=acc,
                 scalar=1.0,
-                in1=volt_sb[:, t * P : (t + 1) * P],
+                in1=volt_sb[:, first : first + width],
                 op0=MULT,
                 op1=MULT,
-                accum_out=parts[:, t : t + 1],
+                accum_out=parts[:, part : part + 1],
             )
 
-        def balance():
-            difference = small.tile([P, K], F32)
+        def balance(h, part):
+            half = slice(h * HALF, (h + 1) * HALF)
+            difference = small.tile([P, HALF], F32, name="difference%d" % h)
             nc.vector.scalar_tensor_tensor(
                 out=difference[:],
-                in0=gens_sb[:],
+                in0=gens_sb[:, half],
                 scalar=-1.0,
-                in1=loads_sb[:],
+                in1=loads_sb[:, half],
                 op0=MULT,
                 op1=ADD,
-                accum_out=parts[:, ROUNDS : ROUNDS + 1],
+                accum_out=parts[:, part : part + 1],
             )
 
-        for step in range(BLOCKS + AHEAD):
-            if step < BLOCKS:
-                flip(step)
-            j = step - AHEAD
-            if j >= 0:
-                quantise(j)
-            if j == BLOCKS - 1:
-                balance()
-            if j >= 2 and j % 2 == 0:
-                multiply(j // 2 - 1)
+        for j in range(BLOCKS - 1):
+            flip(j)
+            quantise(j)
+        flip(BLOCKS - 1)
+        balance(0, 2)
+        quantise(BLOCKS - 1)
+        balance(1, 3)
+
+        acc_early = acc_psum.tile([P, EARLY * P], F32)
+        for t in range(EARLY):
+            multiply(t, acc_early[:, t * P : (t + 1) * P])
+        acc_last = acc_psum.tile([P, P], F32)
+        multiply(EARLY, acc_last[:])
+        weigh(acc_early[:], 0, EARLY * P, 0)
+        weigh(acc_last[:], EARLY * P, P, 1)
 
         total = small.tile([P, 1], F32)
         nc.vector.tensor_reduce(out=total[:], in_=parts[:], axis=mybir.AxisListType.X, op=ADD)
 
-        row_ps = row_psum.tile([P, P], F32)
+        row_ps = acc_psum.tile([P, P], F32)
         nc.tensor.transpose(row_ps[:], total[:, 0:1].to_broadcast([P, P]), ident[:])
         row_sb = small.tile([P, P], F32)
         nc.vector.tensor_copy(out=row_sb[:], in_=row_ps[:])

@@ -20,6 +20,7 @@ ROUNDS = NB // P
 BLOCKS = 1 + 2 * ROUNDS
 EARLY = ROUNDS - 1
 HALF = K // 2
+QUAD = 32
 
 FLOPS = 2 * 2 * P * NB * K
 
@@ -59,6 +60,8 @@ def tile_kktloss_pc_s_kernel(tc, Volt, Y_top, Yconj_top, PQ_Loads, PQ_Gens, out)
         codes = keep.tile([P, BLOCKS, PASSES * P], U32, align_bytes=64)
         scales = keep.tile([P, BLOCKS, PASSES * P], U8, align_bytes=64)
         parts = small.tile([P, 4], F32)
+        column = small.tile([P, QUAD], F32, align_bytes=64)
+        nc.vector.memset(column[:], 0.0)
         grouped = {}
 
         def flip(j):
@@ -133,11 +136,7 @@ def tile_kktloss_pc_s_kernel(tc, Volt, Y_top, Yconj_top, PQ_Loads, PQ_Gens, out)
         weigh(acc_early[:], 0, EARLY * P, 0)
         weigh(acc_last[:], EARLY * P, P, 1)
 
-        total = small.tile([P, 1], F32)
-        nc.vector.tensor_reduce(out=total[:], in_=parts[:], axis=mybir.AxisListType.X, op=ADD)
-
-        row_ps = acc_psum.tile([P, P], F32)
-        nc.tensor.transpose(row_ps[:], total[:, 0:1].to_broadcast([P, P]), ident[:])
-        row_sb = small.tile([P, P], F32)
-        nc.vector.tensor_copy(out=row_sb[:], in_=row_ps[:])
-        nc.sync.dma_start(out=out.rearrange("(o b) -> o b", o=1), in_=row_sb[0:1, :])
+        nc.vector.tensor_reduce(out=column[:, 0:1], in_=parts[:], axis=mybir.AxisListType.X, op=ADD)
+        turned = small.tile([P, QUAD], F32, align_bytes=64)
+        nc.vector.transpose(out=turned[:], in_=column[:])
+        nc.sync.dma_start(out=out.rearrange("(q r) -> q r", r=QUAD), in_=turned[0:P:QUAD, :])

@@ -59,7 +59,8 @@ def tile_kktloss_pc_s_kernel(tc, Volt, Y_top, Yconj_top, PQ_Loads, PQ_Gens, out)
 
         codes = keep.tile([P, BLOCKS, PASSES * P], U32, align_bytes=64)
         scales = keep.tile([P, BLOCKS, PASSES * P], U8, align_bytes=64)
-        parts = small.tile([P, 4], F32)
+        parts = small.tile([P, 16], F32)
+        nc.vector.memset(parts[:], 0.0)
         column = small.tile([P, QUAD], F32, align_bytes=64)
         nc.vector.memset(column[:], 0.0)
         grouped = {}
@@ -107,26 +108,36 @@ def tile_kktloss_pc_s_kernel(tc, Volt, Y_top, Yconj_top, PQ_Loads, PQ_Gens, out)
                 accum_out=parts[:, part : part + 1],
             )
 
-        def balance(h, part):
-            half = slice(h * HALF, (h + 1) * HALF)
-            difference = small.tile([P, HALF], F32, name="difference%d" % h)
+        def balance_on_vector(part):
+            difference = small.tile([P, HALF], F32)
             nc.vector.scalar_tensor_tensor(
                 out=difference[:],
-                in0=gens_sb[:, half],
+                in0=gens_sb[:, 0:HALF],
                 scalar=-1.0,
-                in1=loads_sb[:, half],
+                in1=loads_sb[:, 0:HALF],
                 op0=MULT,
                 op1=ADD,
                 accum_out=parts[:, part : part + 1],
             )
 
+        def balance_on_scalar(part):
+            for n, (source, sign) in enumerate(((loads_sb, 1.0), (gens_sb, -1.0))):
+                signed = small.tile([P, HALF], F32, name="signed%d" % n)
+                nc.scalar.activation(
+                    out=signed[:],
+                    in_=source[:, HALF:K],
+                    func=mybir.ActivationFunctionType.Copy,
+                    scale=sign,
+                    accum_out=parts[:, part + n : part + n + 1],
+                )
+
         for j in range(BLOCKS - 1):
             flip(j)
             quantise(j)
         flip(BLOCKS - 1)
-        balance(0, 2)
+        balance_on_vector(2)
         quantise(BLOCKS - 1)
-        balance(1, 3)
+        balance_on_scalar(8)
 
         acc_early = acc_psum.tile([P, EARLY * P], F32)
         for t in range(EARLY):

@@ -18,7 +18,8 @@ K_PASS = 512
 PASSES = K // K_PASS
 ROUNDS = NB // P
 BLOCKS = 1 + 2 * ROUNDS
-EARLY = ROUNDS - 1
+EARLY = 2
+LEAD = 2
 HALF = K // 2
 QUAD = 32
 
@@ -131,21 +132,21 @@ def tile_kktloss_pc_s_kernel(tc, Volt, Y_top, Yconj_top, PQ_Loads, PQ_Gens, out)
                     accum_out=parts[:, part + n : part + n + 1],
                 )
 
-        for j in range(BLOCKS - 1):
+        for j in range(BLOCKS):
             flip(j)
+            if j == BLOCKS - 1:
+                balance_on_vector(3)
             quantise(j)
-        flip(BLOCKS - 1)
-        balance_on_vector(2)
-        quantise(BLOCKS - 1)
+            if j == 2 * EARLY + LEAD:
+                acc_early = acc_psum.tile([P, EARLY * P], F32)
+                for t in range(EARLY):
+                    multiply(t, acc_early[:, t * P : (t + 1) * P])
+                weigh(acc_early[:], 0, EARLY * P, 0)
         balance_on_scalar(8)
-
-        acc_early = acc_psum.tile([P, EARLY * P], F32)
-        for t in range(EARLY):
-            multiply(t, acc_early[:, t * P : (t + 1) * P])
-        acc_last = acc_psum.tile([P, P], F32)
-        multiply(EARLY, acc_last[:])
-        weigh(acc_early[:], 0, EARLY * P, 0)
-        weigh(acc_last[:], EARLY * P, P, 1)
+        for t in range(EARLY, ROUNDS):
+            acc_late = acc_psum.tile([P, P], F32, name="acc_late%d" % t)
+            multiply(t, acc_late[:])
+            weigh(acc_late[:], t * P, P, t - EARLY + 1)
 
         nc.vector.tensor_reduce(out=column[:, 0:1], in_=parts[:], axis=mybir.AxisListType.X, op=ADD)
         turned = small.tile([P, QUAD], F32, align_bytes=64)

from contextlib import ExitStack

import concourse.mybir as mybir
from concourse.masks import make_identity

F32 = mybir.dt.float32
BF16 = mybir.dt.bfloat16
U32 = mybir.dt.uint32
U8 = mybir.dt.uint8
FP8X4 = mybir.dt.float8_e4m3fn_x4
MULT = mybir.AluOpType.mult
ADD = mybir.AluOpType.add

P = 128
K = 1024
NB = 512
K_PASS = 512
PASSES = K // K_PASS
ROUNDS = NB // P
BLOCKS = 1 + 2 * ROUNDS
EARLY = 2
LEAD = 2
HALF = K // 2
QUAD = 32

FLOPS = 2 * 2 * P * NB * K


def tile_kktloss_pc_s_kernel(tc, Volt, Y_top, Yconj_top, PQ_Loads, PQ_Gens, out):
    nc = tc.nc
    with ExitStack() as ctx:
        consts = ctx.enter_context(tc.tile_pool(name="consts", bufs=1))
        loads = ctx.enter_context(tc.tile_pool(name="loads", bufs=1))
        stage = ctx.enter_context(tc.tile_pool(name="stage", bufs=4))
        keep = ctx.enter_context(tc.tile_pool(name="keep", bufs=1))
        small = ctx.enter_context(tc.tile_pool(name="small", bufs=1))
        flip_psum = ctx.enter_context(tc.psum_pool(name="flip_psum", bufs=5))
        acc_psum = ctx.enter_context(tc.psum_pool(name="acc_psum", bufs=1))
        ctx.enter_context(tc.manual_schedule())

        ident = consts.tile([P, P], F32)
        make_identity(nc, ident[:])

        sources = [Volt[:, :]]
        for t in range(ROUNDS):
            sources.append(Y_top[t * P : (t + 1) * P, :])
            sources.append(Yconj_top[t * P : (t + 1) * P, :])
        rows_sb = []
        for j in range(BLOCKS):
            block = loads.tile([P, K], BF16, name="rows%d" % j)
            nc.sync.dma_start(out=block[:], in_=sources[j])
            rows_sb.append(block)
        volt_sb = rows_sb[0]
        loads_sb = loads.tile([P, K], BF16)
        gens_sb = loads.tile([P, K], BF16)
        for h in range(2):
            half = slice(h * HALF, (h + 1) * HALF)
            nc.sync.dma_start(out=loads_sb[:, half], in_=PQ_Loads[:, half])
            nc.sync.dma_start(out=gens_sb[:, half], in_=PQ_Gens[:, half])

        codes = keep.tile([P, BLOCKS, PASSES * P], U32, align_bytes=64)
        scales = keep.tile([P, BLOCKS, PASSES * P], U8, align_bytes=64)
        parts = small.tile([P, 16], F32)
        nc.vector.memset(parts[:], 0.0)
        column = small.tile([P, QUAD], F32, align_bytes=64)
        nc.vector.memset(column[:], 0.0)
        grouped = {}

        def flip(j):
            words = rows_sb[j][:].bitcast(F32)
            flipped = flip_psum.tile([P, 2 * PASSES, P], F32)
            for s in range(2 * PASSES):
                nc.tensor.transpose(flipped[:, s, :], words[:, s * P : (s + 1) * P], ident[:])
            grouped[j] = stage.tile([P, K], BF16, align_bytes=64, name="grouped")
            nc.scalar.copy(
                out=grouped[j][:].bitcast(F32).rearrange("p (g r u) -> p g r u", g=PASSES, u=2),
                in_=flipped[:].rearrange("p (g u) r -> p g r u", u=2),
            )

        def quantise(j):
            nc.vector.quantize_mx(
                out=codes[:, j, :].bitcast(FP8X4), scales=scales[:, j, :], in_=grouped[j][:]
            )

        def multiply(t, acc):
            for which in range(2):
                j = 1 + 2 * t + which
                for g in range(PASSES):
                    cols = slice(g * P, (g + 1) * P)
                    nc.tensor.matmul_mx(
                        out=acc,
                        lhsT=codes[:, 0, cols].bitcast(FP8X4),
                        lhsT_scale=scales[:, 0, cols],
                        rhs=codes[:, j, cols].bitcast(FP8X4),
                        rhs_scale=scales[:, j, cols],
                        start=(which == 0 and g == 0),
                        stop=(which == 1 and g == PASSES - 1),
                    )

        def weigh(acc, first, width, part):
            weighted = small.tile([P, width], F32, name="weighted%d" % part)
            nc.vector.scalar_tensor_tensor(
                out=weighted[:],
                in0=acc,
                scalar=1.0,
                in1=volt_sb[:, first : first + width],
                op0=MULT,
                op1=MULT,
                accum_out=parts[:, part : part + 1],
            )

        def balance_on_vector(part):
            difference = small.tile([P, HALF], F32)
            nc.vector.scalar_tensor_tensor(
                out=difference[:],
                in0=gens_sb[:, 0:HALF],
                scalar=-1.0,
                in1=loads_sb[:, 0:HALF],
                op0=MULT,
                op1=ADD,
                accum_out=parts[:, part : part + 1],
            )

        def balance_on_scalar(part):
            for n, (source, sign) in enumerate(((loads_sb, 1.0), (gens_sb, -1.0))):
                signed = small.tile([P, HALF], F32, name="signed%d" % n)
                nc.scalar.activation(
                    out=signed[:],
                    in_=source[:, HALF:K],
                    func=mybir.ActivationFunctionType.Copy,
                    scale=sign,
                    accum_out=parts[:, part + n : part + n + 1],
                )

        for j in range(BLOCKS):
            flip(j)
            if j == BLOCKS - 1:
                balance_on_vector(3)
            quantise(j)
            if j == 2 * EARLY + LEAD:
                acc_early = acc_psum.tile([P, EARLY * P], F32)
                for t in range(EARLY):
                    multiply(t, acc_early[:, t * P : (t + 1) * P])
                weigh(acc_early[:], 0, EARLY * P, 0)
        balance_on_scalar(8)
        for t in range(EARLY, ROUNDS):
            acc_late = acc_psum.tile([P, P], F32, name="acc_late%d" % t)
            multiply(t, acc_late[:])
            weigh(acc_late[:], t * P, P, t - EARLY + 1)

        nc.vector.tensor_reduce(out=column[:, 0:1], in_=parts[:], axis=mybir.AxisListType.X, op=ADD)
        turned = small.tile([P, QUAD], F32, align_bytes=64)
        nc.vector.transpose(out=turned[:], in_=column[:])
        nc.sync.dma_start(out=out.rearrange("(q r) -> q r", r=QUAD), in_=turned[0:P:QUAD, :])
